import numpy as np
import ml_dtypes

BF16 = ml_dtypes.bfloat16


def bf(x):
    return np.asarray(x, np.float32).astype(BF16)


def f32(x):
    return np.asarray(x, np.float32)


def f64(x):
    return np.asarray(x).astype(np.float64)


def striped(idx):
    return np.tile(idx.reshape(-1, 16).T, (8, 1))


S, D, H, M, K, N = 2048, 128, 128, 512, 512, 512


def sigmoid(v):
    return 1.0 / (1.0 + np.exp(-v))


def setup_inputs():
    return {"table": bf(np.random.standard_normal((S, D))), "w_p": bf(0.7 * np.random.standard_normal((D, M)) / np.sqrt(D)), "ctx": bf(np.random.standard_normal((K, N))), "w_ctx": bf(0.7 * np.random.standard_normal((K, M)) / np.sqrt(K)), "h0": bf(np.random.standard_normal((H, N))), "u": bf(0.7 * np.random.standard_normal((H, M)) / np.sqrt(H)), "c0": f32(np.random.standard_normal((H, N))), "b": f32(0.1 * np.random.standard_normal((M, 1))), "offs": striped(np.random.permutation(np.tile(np.arange(S), 2))[:N])}


def reference(table, w_p, ctx, w_ctx, h0, u, c0, b, offs):
    idx = offs[:16].T.reshape(-1)
    z = f64(w_p).T @ f64(table)[idx].T + f64(w_ctx).T @ f64(ctx) + f64(u).T @ f64(h0) + f64(b)
    zi, zf, zu, zo = z[:H], z[H:2 * H], z[2 * H:3 * H], z[3 * H:]
    c1 = sigmoid(zf) * f64(c0) + sigmoid(zi) * np.maximum(zu, 0.0)
    h1 = sigmoid(zo) * np.maximum(c1, 0.0)
    return np.concatenate([h1, c1], axis=0)

@@ -1,0 +1,99 @@
+import concourse.mybir as mybir
+from concourse.masks import make_identity
+
+BF16 = mybir.dt.bfloat16
+F32 = mybir.dt.float32
+U16 = mybir.dt.uint16
+FUNC = mybir.ActivationFunctionType
+ALU = mybir.AluOpType
+
+P = 128
+SPEAKERS = 2048
+SAMPLES = 512
+CTX_BLOCKS = 4
+QUARTER = 4 * P
+GATE_I, GATE_F, GATE_U, GATE_O = 0, 1, 2, 3
+
+FLOPS = 2 * 512 * SAMPLES * (P + CTX_BLOCKS * P + P)
+
+
+def tile_test_target_kernel(tc, table, w_p, ctx, w_ctx, h0, u, c0, b, offs, out):
+    nc = tc.nc
+    with (
+        tc.tile_pool(name="held", bufs=1) as held,
+        tc.psum_pool(name="flip", bufs=4) as flip,
+        tc.psum_pool(name="gates", bufs=1) as gates,
+    ):
+        offsets = held.tile([P, SAMPLES // 16], U16, name="offsets")
+        nc.sync.dma_start(offsets[:], offs)
+
+        table_blocks = table.rearrange("(t p) d -> p t d", p=P)
+        rows = []
+        for q in range(4):
+            rows_q = held.tile([P, 4, P], BF16, name=f"rows{q}")
+            queue = nc.sync if q % 2 == 0 else nc.scalar
+            queue.dma_start(rows_q[:], table_blocks[:, 4 * q : 4 * (q + 1), :])
+            rows.append(rows_q)
+
+        w_p_sb = held.tile([P, 4 * P], BF16, name="w_p_sb")
+        nc.sync.dma_start(w_p_sb[:], w_p)
+        w_ctx_sb = held.tile([P, CTX_BLOCKS, 4 * P], BF16, name="w_ctx_sb")
+        nc.scalar.dma_start(w_ctx_sb[:], w_ctx.rearrange("(k p) m -> p k m", p=P))
+        ctx_sb = held.tile([P, CTX_BLOCKS, SAMPLES], BF16, name="ctx_sb")
+        nc.sync.dma_start(ctx_sb[:], ctx.rearrange("(k p) j -> p k j", p=P))
+        u_sb = held.tile([P, 4 * P], BF16, name="u_sb")
+        nc.scalar.dma_start(u_sb[:], u)
+        h0_sb = held.tile([P, SAMPLES], BF16, name="h0_sb")
+        nc.sync.dma_start(h0_sb[:], h0)
+        c0_sb = held.tile([P, SAMPLES], F32, name="c0_sb")
+        nc.scalar.dma_start(c0_sb[:], c0)
+        b_sb = held.tile([P, 4], F32, name="b_sb")
+        with nc.allow_non_contiguous_dma(reason="512 floats, one to a partition and gate"):
+            nc.sync.dma_start(b_sb[:], b.rearrange("(g p) o -> p (g o)", p=P))
+
+        identity = held.tile([P, P], BF16, name="identity")
+        make_identity(nc, identity[:])
+        speakers = held.tile([P, SPEAKERS], BF16, name="speakers")
+        for q in range(4):
+            flipped = flip.tile([P, QUARTER], BF16, name="flipped")
+            for t in range(4):
+                nc.tensor.transpose(flipped[:, t * P : (t + 1) * P], rows[q][:, t, :], identity[:])
+            nc.vector.tensor_copy(speakers[:, q * QUARTER : (q + 1) * QUARTER], flipped[:])
+
+        z = [gates.tile([P, SAMPLES], F32, name=f"z{g}") for g in range(4)]
+        for g in range(4):
+            nc.tensor.matmul(
+                z[g][:],
+                w_p_sb[:, g * P : (g + 1) * P],
+                speakers[:].indirect(offsets[:]),
+                start=True,
+                stop=False,
+            )
+        for g in (GATE_F, GATE_I, GATE_U, GATE_O):
+            for k in range(CTX_BLOCKS):
+                nc.tensor.matmul(
+                    z[g][:], w_ctx_sb[:, k, g * P : (g + 1) * P], ctx_sb[:, k, :], start=False, stop=False
+                )
+            nc.tensor.matmul(z[g][:], u_sb[:, g * P : (g + 1) * P], h0_sb[:], start=False, stop=True)
+
+        def bias(g):
+            return b_sb[:, g : g + 1]
+
+        forget = held.tile([P, SAMPLES], F32, name="forget")
+        nc.scalar.activation(forget[:], z[GATE_F][:], FUNC.Sigmoid, bias=bias(GATE_F))
+        kept = held.tile([P, SAMPLES], F32, name="kept")
+        nc.vector.tensor_tensor(kept[:], forget[:], c0_sb[:], ALU.mult)
+
+        admit = held.tile([P, SAMPLES], F32, name="admit")
+        nc.scalar.activation(admit[:], z[GATE_I][:], FUNC.Sigmoid, bias=bias(GATE_I))
+        fresh = held.tile([P, SAMPLES], F32, name="fresh")
+        nc.vector.scalar_tensor_tensor(fresh[:], z[GATE_U][:], bias(GATE_U), admit[:], ALU.add, ALU.mult)
+        c1 = held.tile([P, SAMPLES], F32, name="c1")
+        nc.vector.scalar_tensor_tensor(c1[:], fresh[:], 0.0, kept[:], ALU.max, ALU.add)
+        nc.sync.dma_start(out[P : 2 * P, :], c1[:])
+
+        expose = held.tile([P, SAMPLES], F32, name="expose")
+        nc.scalar.activation(expose[:], z[GATE_O][:], FUNC.Sigmoid, bias=bias(GATE_O))
+        h1 = held.tile([P, SAMPLES], F32, name="h1")
+        nc.vector.scalar_tensor_tensor(h1[:], c1[:], 0.0, expose[:], ALU.max, ALU.mult)
+        nc.sync.dma_start(out[0:P, :], h1[:])

@@ -10,9 +10,11 @@ ALU = mybir.AluOpType
 P = 128
 SPEAKERS = 2048
 SAMPLES = 512
+HALF = SAMPLES // 2
 CTX_BLOCKS = 4
 QUARTER = 4 * P
 GATE_I, GATE_F, GATE_U, GATE_O = 0, 1, 2, 3
+GATE_ORDER = (GATE_F, GATE_I, GATE_U, GATE_O)
 
 FLOPS = 2 * 512 * SAMPLES * (P + CTX_BLOCKS * P + P)
 
@@ -24,8 +26,14 @@ def tile_test_target_kernel(tc, table, w_p, ctx, w_ctx, h0, u, c0, b, offs, out)
         tc.psum_pool(name="flip", bufs=4) as flip,
         tc.psum_pool(name="gates", bufs=1) as gates,
     ):
-        offsets = held.tile([P, SAMPLES // 16], U16, name="offsets")
-        nc.sync.dma_start(offsets[:], offs)
+        ctx_sb, w_ctx_sb = [], []
+        for k in range(CTX_BLOCKS):
+            ctx_k = held.tile([P, SAMPLES], BF16, name=f"ctx{k}")
+            nc.sync.dma_start(ctx_k[:], ctx[k * P : (k + 1) * P, :])
+            ctx_sb.append(ctx_k)
+            w_ctx_k = held.tile([P, 4 * P], BF16, name=f"w_ctx{k}")
+            nc.scalar.dma_start(w_ctx_k[:], w_ctx[k * P : (k + 1) * P, :])
+            w_ctx_sb.append(w_ctx_k)
 
         table_blocks = table.rearrange("(t p) d -> p t d", p=P)
         rows = []
@@ -35,21 +43,30 @@ def tile_test_target_kernel(tc, table, w_p, ctx, w_ctx, h0, u, c0, b, offs, out)
             queue.dma_start(rows_q[:], table_blocks[:, 4 * q : 4 * (q + 1), :])
             rows.append(rows_q)
 
-        w_p_sb = held.tile([P, 4 * P], BF16, name="w_p_sb")
-        nc.sync.dma_start(w_p_sb[:], w_p)
-        w_ctx_sb = held.tile([P, CTX_BLOCKS, 4 * P], BF16, name="w_ctx_sb")
-        nc.scalar.dma_start(w_ctx_sb[:], w_ctx.rearrange("(k p) m -> p k m", p=P))
-        ctx_sb = held.tile([P, CTX_BLOCKS, SAMPLES], BF16, name="ctx_sb")
-        nc.sync.dma_start(ctx_sb[:], ctx.rearrange("(k p) j -> p k j", p=P))
-        u_sb = held.tile([P, 4 * P], BF16, name="u_sb")
-        nc.scalar.dma_start(u_sb[:], u)
         h0_sb = held.tile([P, SAMPLES], BF16, name="h0_sb")
         nc.sync.dma_start(h0_sb[:], h0)
+        u_sb = held.tile([P, 4 * P], BF16, name="u_sb")
+        nc.scalar.dma_start(u_sb[:], u)
+        offsets = held.tile([P, SAMPLES // 16], U16, name="offsets")
+        nc.sync.dma_start(offsets[:], offs)
+        w_p_sb = held.tile([P, 4 * P], BF16, name="w_p_sb")
+        nc.scalar.dma_start(w_p_sb[:], w_p)
         c0_sb = held.tile([P, SAMPLES], F32, name="c0_sb")
-        nc.scalar.dma_start(c0_sb[:], c0)
+        nc.sync.dma_start(c0_sb[:], c0)
         b_sb = held.tile([P, 4], F32, name="b_sb")
         with nc.allow_non_contiguous_dma(reason="512 floats, one to a partition and gate"):
-            nc.sync.dma_start(b_sb[:], b.rearrange("(g p) o -> p (g o)", p=P))
+            nc.scalar.dma_start(b_sb[:], b.rearrange("(g p) o -> p (g o)", p=P))
+
+        z = [gates.tile([P, SAMPLES], F32, name=f"z{g}") for g in range(4)]
+
+        def gate_columns(g):
+            return slice(g * P, (g + 1) * P)
+
+        for k in range(CTX_BLOCKS):
+            for g in GATE_ORDER:
+                nc.tensor.matmul(
+                    z[g][:], w_ctx_sb[k][:, gate_columns(g)], ctx_sb[k][:], start=(k == 0), stop=False
+                )
 
         identity = held.tile([P, P], BF16, name="identity")
         make_identity(nc, identity[:])
@@ -60,21 +77,18 @@ def tile_test_target_kernel(tc, table, w_p, ctx, w_ctx, h0, u, c0, b, offs, out)
                 nc.tensor.transpose(flipped[:, t * P : (t + 1) * P], rows[q][:, t, :], identity[:])
             nc.vector.tensor_copy(speakers[:, q * QUARTER : (q + 1) * QUARTER], flipped[:])
 
-        z = [gates.tile([P, SAMPLES], F32, name=f"z{g}") for g in range(4)]
-        for g in range(4):
-            nc.tensor.matmul(
-                z[g][:],
-                w_p_sb[:, g * P : (g + 1) * P],
-                speakers[:].indirect(offsets[:]),
-                start=True,
-                stop=False,
-            )
-        for g in (GATE_F, GATE_I, GATE_U, GATE_O):
-            for k in range(CTX_BLOCKS):
+        for g in GATE_ORDER:
+            nc.tensor.matmul(z[g][:], u_sb[:, gate_columns(g)], h0_sb[:], start=False, stop=False)
+
+        for g in GATE_ORDER:
+            for half in range(2):
                 nc.tensor.matmul(
-                    z[g][:], w_ctx_sb[:, k, g * P : (g + 1) * P], ctx_sb[:, k, :], start=False, stop=False
+                    z[g][:, half * HALF : (half + 1) * HALF],
+                    w_p_sb[:, gate_columns(g)],
+                    speakers[:].indirect(offsets[:, half * (HALF // 16) : (half + 1) * (HALF // 16)]),
+                    start=False,
+                    stop=(half == 1),
                 )
-            nc.tensor.matmul(z[g][:], u_sb[:, g * P : (g + 1) * P], h0_sb[:], start=False, stop=True)
 
         def bias(g):
             return b_sb[:, g : g + 1]

@@ -23,25 +23,22 @@ def tile_test_target_kernel(tc, table, w_p, ctx, w_ctx, h0, u, c0, b, offs, out)
     nc = tc.nc
     with (
         tc.tile_pool(name="held", bufs=1) as held,
-        tc.psum_pool(name="flip", bufs=4) as flip,
+        tc.psum_pool(name="flip", bufs=2) as flip,
         tc.psum_pool(name="gates", bufs=1) as gates,
     ):
-        ctx_sb, w_ctx_sb = [], []
-        for k in range(CTX_BLOCKS):
-            ctx_k = held.tile([P, SAMPLES], BF16, name=f"ctx{k}")
-            nc.sync.dma_start(ctx_k[:], ctx[k * P : (k + 1) * P, :])
-            ctx_sb.append(ctx_k)
-            w_ctx_k = held.tile([P, 4 * P], BF16, name=f"w_ctx{k}")
-            nc.scalar.dma_start(w_ctx_k[:], w_ctx[k * P : (k + 1) * P, :])
-            w_ctx_sb.append(w_ctx_k)
-
         table_blocks = table.rearrange("(t p) d -> p t d", p=P)
-        rows = []
-        for q in range(4):
-            rows_q = held.tile([P, 4, P], BF16, name=f"rows{q}")
-            queue = nc.sync if q % 2 == 0 else nc.scalar
-            queue.dma_start(rows_q[:], table_blocks[:, 4 * q : 4 * (q + 1), :])
-            rows.append(rows_q)
+        ctx_sb, w_ctx_sb, rows = [], [], []
+        for s in range(CTX_BLOCKS):
+            ctx_s = held.tile([P, SAMPLES], BF16, name=f"ctx{s}")
+            nc.sync.dma_start(ctx_s[:], ctx[s * P : (s + 1) * P, :])
+            ctx_sb.append(ctx_s)
+            w_ctx_s = held.tile([P, 4 * P], BF16, name=f"w_ctx{s}")
+            nc.scalar.dma_start(w_ctx_s[:], w_ctx[s * P : (s + 1) * P, :])
+            w_ctx_sb.append(w_ctx_s)
+            rows_s = held.tile([P, 4, P], BF16, name=f"rows{s}")
+            queue = nc.sync if s % 2 == 0 else nc.scalar
+            queue.dma_start(rows_s[:], table_blocks[:, 4 * s : 4 * (s + 1), :])
+            rows.append(rows_s)
 
         h0_sb = held.tile([P, SAMPLES], BF16, name="h0_sb")
         nc.sync.dma_start(h0_sb[:], h0)
@@ -62,20 +59,18 @@ def tile_test_target_kernel(tc, table, w_p, ctx, w_ctx, h0, u, c0, b, offs, out)
         def gate_columns(g):
             return slice(g * P, (g + 1) * P)
 
-        for k in range(CTX_BLOCKS):
-            for g in GATE_ORDER:
-                nc.tensor.matmul(
-                    z[g][:], w_ctx_sb[k][:, gate_columns(g)], ctx_sb[k][:], start=(k == 0), stop=False
-                )
-
         identity = held.tile([P, P], BF16, name="identity")
         make_identity(nc, identity[:])
         speakers = held.tile([P, SPEAKERS], BF16, name="speakers")
-        for q in range(4):
+        for s in range(CTX_BLOCKS):
+            for g in GATE_ORDER:
+                nc.tensor.matmul(
+                    z[g][:], w_ctx_sb[s][:, gate_columns(g)], ctx_sb[s][:], start=(s == 0), stop=False
+                )
             flipped = flip.tile([P, QUARTER], BF16, name="flipped")
             for t in range(4):
-                nc.tensor.transpose(flipped[:, t * P : (t + 1) * P], rows[q][:, t, :], identity[:])
-            nc.vector.tensor_copy(speakers[:, q * QUARTER : (q + 1) * QUARTER], flipped[:])
+                nc.tensor.transpose(flipped[:, t * P : (t + 1) * P], rows[s][:, t, :], identity[:])
+            nc.vector.tensor_copy(speakers[:, s * QUARTER : (s + 1) * QUARTER], flipped[:])
 
         for g in GATE_ORDER:
             nc.tensor.matmul(z[g][:], u_sb[:, gate_columns(g)], h0_sb[:], start=False, stop=False)

@@ -23,22 +23,28 @@ def tile_test_target_kernel(tc, table, w_p, ctx, w_ctx, h0, u, c0, b, offs, out)
     nc = tc.nc
     with (
         tc.tile_pool(name="held", bufs=1) as held,
-        tc.psum_pool(name="flip", bufs=2) as flip,
+        tc.psum_pool(name="flip", bufs=4) as flip,
         tc.psum_pool(name="gates", bufs=1) as gates,
     ):
+        identity = held.tile([P, P], BF16, name="identity")
+        make_identity(nc, identity[:])
+
         table_blocks = table.rearrange("(t p) d -> p t d", p=P)
-        ctx_sb, w_ctx_sb, rows = [], [], []
-        for s in range(CTX_BLOCKS):
-            ctx_s = held.tile([P, SAMPLES], BF16, name=f"ctx{s}")
-            nc.sync.dma_start(ctx_s[:], ctx[s * P : (s + 1) * P, :])
-            ctx_sb.append(ctx_s)
-            w_ctx_s = held.tile([P, 4 * P], BF16, name=f"w_ctx{s}")
-            nc.scalar.dma_start(w_ctx_s[:], w_ctx[s * P : (s + 1) * P, :])
-            w_ctx_sb.append(w_ctx_s)
-            rows_s = held.tile([P, 4, P], BF16, name=f"rows{s}")
-            queue = nc.sync if s % 2 == 0 else nc.scalar
-            queue.dma_start(rows_s[:], table_blocks[:, 4 * s : 4 * (s + 1), :])
-            rows.append(rows_s)
+        rows = []
+        for q in range(4):
+            rows_q = held.tile([P, 4, P], BF16, name=f"rows{q}")
+            queue = nc.sync if q % 2 == 0 else nc.scalar
+            queue.dma_start(rows_q[:], table_blocks[:, 4 * q : 4 * (q + 1), :])
+            rows.append(rows_q)
+
+        ctx_sb, w_ctx_sb = [], []
+        for k in range(CTX_BLOCKS):
+            ctx_k = held.tile([P, SAMPLES], BF16, name=f"ctx{k}")
+            nc.sync.dma_start(ctx_k[:], ctx[k * P : (k + 1) * P, :])
+            ctx_sb.append(ctx_k)
+            w_ctx_k = held.tile([P, 4 * P], BF16, name=f"w_ctx{k}")
+            nc.scalar.dma_start(w_ctx_k[:], w_ctx[k * P : (k + 1) * P, :])
+            w_ctx_sb.append(w_ctx_k)
 
         h0_sb = held.tile([P, SAMPLES], BF16, name="h0_sb")
         nc.sync.dma_start(h0_sb[:], h0)
@@ -48,29 +54,30 @@ def tile_test_target_kernel(tc, table, w_p, ctx, w_ctx, h0, u, c0, b, offs, out)
         nc.sync.dma_start(offsets[:], offs)
         w_p_sb = held.tile([P, 4 * P], BF16, name="w_p_sb")
         nc.scalar.dma_start(w_p_sb[:], w_p)
+
         c0_sb = held.tile([P, SAMPLES], F32, name="c0_sb")
-        nc.sync.dma_start(c0_sb[:], c0)
+        nc.gpsimd.dma_start(c0_sb[:], c0)
         b_sb = held.tile([P, 4], F32, name="b_sb")
         with nc.allow_non_contiguous_dma(reason="512 floats, one to a partition and gate"):
-            nc.scalar.dma_start(b_sb[:], b.rearrange("(g p) o -> p (g o)", p=P))
+            nc.gpsimd.dma_start(b_sb[:], b.rearrange("(g p) o -> p (g o)", p=P))
+
+        speakers = held.tile([P, SPEAKERS], BF16, name="speakers")
+        for q in range(4):
+            flipped = flip.tile([P, QUARTER], BF16, name="flipped")
+            for t in range(4):
+                nc.tensor.transpose(flipped[:, t * P : (t + 1) * P], rows[q][:, t, :], identity[:])
+            nc.vector.tensor_copy(speakers[:, q * QUARTER : (q + 1) * QUARTER], flipped[:])
 
         z = [gates.tile([P, SAMPLES], F32, name=f"z{g}") for g in range(4)]
 
         def gate_columns(g):
             return slice(g * P, (g + 1) * P)
 
-        identity = held.tile([P, P], BF16, name="identity")
-        make_identity(nc, identity[:])
-        speakers = held.tile([P, SPEAKERS], BF16, name="speakers")
-        for s in range(CTX_BLOCKS):
+        for k in range(CTX_BLOCKS):
             for g in GATE_ORDER:
                 nc.tensor.matmul(
-                    z[g][:], w_ctx_sb[s][:, gate_columns(g)], ctx_sb[s][:], start=(s == 0), stop=False
+                    z[g][:], w_ctx_sb[k][:, gate_columns(g)], ctx_sb[k][:], start=(k == 0), stop=False
                 )
-            flipped = flip.tile([P, QUARTER], BF16, name="flipped")
-            for t in range(4):
-                nc.tensor.transpose(flipped[:, t * P : (t + 1) * P], rows[s][:, t, :], identity[:])
-            nc.vector.tensor_copy(speakers[:, s * QUARTER : (s + 1) * QUARTER], flipped[:])
 
         for g in GATE_ORDER:
             nc.tensor.matmul(z[g][:], u_sb[:, gate_columns(g)], h0_sb[:], start=False, stop=False)

@@ -15,6 +15,7 @@ CTX_BLOCKS = 4
 QUARTER = 4 * P
 GATE_I, GATE_F, GATE_U, GATE_O = 0, 1, 2, 3
 GATE_ORDER = (GATE_F, GATE_I, GATE_U, GATE_O)
+WARM_UP = 3
 
 FLOPS = 2 * 512 * SAMPLES * (P + CTX_BLOCKS * P + P)
 
@@ -23,19 +24,17 @@ def tile_test_target_kernel(tc, table, w_p, ctx, w_ctx, h0, u, c0, b, offs, out)
     nc = tc.nc
     with (
         tc.tile_pool(name="held", bufs=1) as held,
-        tc.psum_pool(name="flip", bufs=4) as flip,
         tc.psum_pool(name="gates", bufs=1) as gates,
+        tc.psum_pool(name="turns", bufs=4) as turns,
     ):
+        zeros = held.tile([P, SAMPLES], BF16, name="zeros")
+        nc.gpsimd.memset(zeros[:], 0.0)
+        unread = gates.tile([P, SAMPLES], F32, name="unread")
+        for i in range(WARM_UP):
+            nc.tensor.matmul(unread[:], zeros[:, 0:P], zeros[:], start=True, stop=True)
+
         identity = held.tile([P, P], BF16, name="identity")
         make_identity(nc, identity[:])
-
-        table_blocks = table.rearrange("(t p) d -> p t d", p=P)
-        rows = []
-        for q in range(4):
-            rows_q = held.tile([P, 4, P], BF16, name=f"rows{q}")
-            queue = nc.sync if q % 2 == 0 else nc.scalar
-            queue.dma_start(rows_q[:], table_blocks[:, 4 * q : 4 * (q + 1), :])
-            rows.append(rows_q)
 
         ctx_sb, w_ctx_sb = [], []
         for k in range(CTX_BLOCKS):
@@ -45,42 +44,53 @@ def tile_test_target_kernel(tc, table, w_p, ctx, w_ctx, h0, u, c0, b, offs, out)
             w_ctx_k = held.tile([P, 4 * P], BF16, name=f"w_ctx{k}")
             nc.scalar.dma_start(w_ctx_k[:], w_ctx[k * P : (k + 1) * P, :])
             w_ctx_sb.append(w_ctx_k)
-
         h0_sb = held.tile([P, SAMPLES], BF16, name="h0_sb")
         nc.sync.dma_start(h0_sb[:], h0)
         u_sb = held.tile([P, 4 * P], BF16, name="u_sb")
         nc.scalar.dma_start(u_sb[:], u)
+
+        table_blocks = table.rearrange("(t p) d -> p t d", p=P)
+        rows = []
+        for q in range(4):
+            rows_q = held.tile([P, 4, P], BF16, name=f"rows{q}")
+            queue = nc.sync if q % 2 == 0 else nc.scalar
+            queue.dma_start(rows_q[:], table_blocks[:, 4 * q : 4 * (q + 1), :])
+            rows.append(rows_q)
+
         offsets = held.tile([P, SAMPLES // 16], U16, name="offsets")
         nc.sync.dma_start(offsets[:], offs)
         w_p_sb = held.tile([P, 4 * P], BF16, name="w_p_sb")
         nc.scalar.dma_start(w_p_sb[:], w_p)
-
         c0_sb = held.tile([P, SAMPLES], F32, name="c0_sb")
-        nc.gpsimd.dma_start(c0_sb[:], c0)
+        nc.sync.dma_start(c0_sb[:], c0)
         b_sb = held.tile([P, 4], F32, name="b_sb")
         with nc.allow_non_contiguous_dma(reason="512 floats, one to a partition and gate"):
-            nc.gpsimd.dma_start(b_sb[:], b.rearrange("(g p) o -> p (g o)", p=P))
-
-        speakers = held.tile([P, SPEAKERS], BF16, name="speakers")
-        for q in range(4):
-            flipped = flip.tile([P, QUARTER], BF16, name="flipped")
-            for t in range(4):
-                nc.tensor.transpose(flipped[:, t * P : (t + 1) * P], rows[q][:, t, :], identity[:])
-            nc.vector.tensor_copy(speakers[:, q * QUARTER : (q + 1) * QUARTER], flipped[:])
-
-        z = [gates.tile([P, SAMPLES], F32, name=f"z{g}") for g in range(4)]
+            nc.scalar.dma_start(b_sb[:], b.rearrange("(g p) o -> p (g o)", p=P))
 
         def gate_columns(g):
             return slice(g * P, (g + 1) * P)
 
-        for k in range(CTX_BLOCKS):
-            for g in GATE_ORDER:
+        def context_and_hidden(z_g, g):
+            for k in range(CTX_BLOCKS):
                 nc.tensor.matmul(
-                    z[g][:], w_ctx_sb[k][:, gate_columns(g)], ctx_sb[k][:], start=(k == 0), stop=False
+                    z_g[:], w_ctx_sb[k][:, gate_columns(g)], ctx_sb[k][:], start=(k == 0), stop=False
                 )
+            nc.tensor.matmul(z_g[:], u_sb[:, gate_columns(g)], h0_sb[:], start=False, stop=False)
 
-        for g in GATE_ORDER:
-            nc.tensor.matmul(z[g][:], u_sb[:, gate_columns(g)], h0_sb[:], start=False, stop=False)
+        z = {}
+        for g in (GATE_F, GATE_I, GATE_U):
+            z[g] = gates.tile([P, SAMPLES], F32, name=f"z{g}")
+            context_and_hidden(z[g], g)
+
+        speakers = held.tile([P, SPEAKERS], BF16, name="speakers")
+        for q in range(4):
+            flipped = turns.tile([P, QUARTER], BF16, name="flipped", tag="turn")
+            for t in range(4):
+                nc.tensor.transpose(flipped[:, t * P : (t + 1) * P], rows[q][:, t, :], identity[:])
+            nc.vector.tensor_copy(speakers[:, q * QUARTER : (q + 1) * QUARTER], flipped[:])
+
+        z[GATE_O] = turns.tile([P, SAMPLES], F32, name="z_o", tag="turn")
+        context_and_hidden(z[GATE_O], GATE_O)
 
         for g in GATE_ORDER:
             for half in range(2):

@@ -70,17 +70,31 @@ def tile_test_target_kernel(tc, table, w_p, ctx, w_ctx, h0, u, c0, b, offs, out)
         def gate_columns(g):
             return slice(g * P, (g + 1) * P)
 
-        def context_and_hidden(z_g, g):
-            for k in range(CTX_BLOCKS):
-                nc.tensor.matmul(
-                    z_g[:], w_ctx_sb[k][:, gate_columns(g)], ctx_sb[k][:], start=(k == 0), stop=False
-                )
-            nc.tensor.matmul(z_g[:], u_sb[:, gate_columns(g)], h0_sb[:], start=False, stop=False)
-
         z = {}
+
+        def context(g, blocks):
+            for k in blocks:
+                nc.tensor.matmul(
+                    z[g][:], w_ctx_sb[k][:, gate_columns(g)], ctx_sb[k][:], start=(k == 0), stop=False
+                )
+
+        def hidden(g, last):
+            nc.tensor.matmul(z[g][:], u_sb[:, gate_columns(g)], h0_sb[:], start=False, stop=last)
+
+        def looked_up(g, last):
+            for half in range(2):
+                nc.tensor.matmul(
+                    z[g][:, half * HALF : (half + 1) * HALF],
+                    w_p_sb[:, gate_columns(g)],
+                    speakers[:].indirect(offsets[:, half * (HALF // 16) : (half + 1) * (HALF // 16)]),
+                    start=False,
+                    stop=(last and half == 1),
+                )
+
         for g in (GATE_F, GATE_I, GATE_U):
             z[g] = gates.tile([P, SAMPLES], F32, name=f"z{g}")
-            context_and_hidden(z[g], g)
+            context(g, range(CTX_BLOCKS))
+            hidden(g, last=False)
 
         speakers = held.tile([P, SPEAKERS], BF16, name="speakers")
         for q in range(4):
@@ -90,17 +104,11 @@ def tile_test_target_kernel(tc, table, w_p, ctx, w_ctx, h0, u, c0, b, offs, out)
             nc.vector.tensor_copy(speakers[:, q * QUARTER : (q + 1) * QUARTER], flipped[:])
 
         z[GATE_O] = turns.tile([P, SAMPLES], F32, name="z_o", tag="turn")
-        context_and_hidden(z[GATE_O], GATE_O)
-
+        context(GATE_O, range(CTX_BLOCKS - 1))
         for g in GATE_ORDER:
-            for half in range(2):
-                nc.tensor.matmul(
-                    z[g][:, half * HALF : (half + 1) * HALF],
-                    w_p_sb[:, gate_columns(g)],
-                    speakers[:].indirect(offsets[:, half * (HALF // 16) : (half + 1) * (HALF // 16)]),
-                    start=False,
-                    stop=(half == 1),
-                )
+            looked_up(g, last=(g != GATE_O))
+        context(GATE_O, [CTX_BLOCKS - 1])
+        hidden(GATE_O, last=True)
 
         def bias(g):
             return b_sb[:, g : g + 1]
@@ -119,7 +127,10 @@ def tile_test_target_kernel(tc, table, w_p, ctx, w_ctx, h0, u, c0, b, offs, out)
         nc.sync.dma_start(out[P : 2 * P, :], c1[:])
 
         expose = held.tile([P, SAMPLES], F32, name="expose")
-        nc.scalar.activation(expose[:], z[GATE_O][:], FUNC.Sigmoid, bias=bias(GATE_O))
         h1 = held.tile([P, SAMPLES], F32, name="h1")
-        nc.vector.scalar_tensor_tensor(h1[:], c1[:], 0.0, expose[:], ALU.max, ALU.mult)
-        nc.sync.dma_start(out[0:P, :], h1[:])
+        for half in range(2):
+            cols = slice(half * HALF, (half + 1) * HALF)
+            nc.scalar.activation(expose[:, cols], z[GATE_O][:, cols], FUNC.Sigmoid, bias=bias(GATE_O))
+            nc.vector.scalar_tensor_tensor(h1[:, cols], c1[:, cols], 0.0, expose[:, cols], ALU.max, ALU.mult)
+            queue = nc.scalar if half == 0 else nc.sync
+            queue.dma_start(out[0:P, cols], h1[:, cols])

@@ -65,7 +65,7 @@ def tile_test_target_kernel(tc, table, w_p, ctx, w_ctx, h0, u, c0, b, offs, out)
         nc.sync.dma_start(c0_sb[:], c0)
         b_sb = held.tile([P, 4], F32, name="b_sb")
         with nc.allow_non_contiguous_dma(reason="512 floats, one to a partition and gate"):
-            nc.scalar.dma_start(b_sb[:], b.rearrange("(g p) o -> p (g o)", p=P))
+            nc.gpsimd.dma_start(b_sb[:], b.rearrange("(g p) o -> p (g o)", p=P))
 
         def gate_columns(g):
             return slice(g * P, (g + 1) * P)

import concourse.mybir as mybir
from concourse.masks import make_identity

BF16 = mybir.dt.bfloat16
F32 = mybir.dt.float32
U16 = mybir.dt.uint16
FUNC = mybir.ActivationFunctionType
ALU = mybir.AluOpType

P = 128
SPEAKERS = 2048
SAMPLES = 512
HALF = SAMPLES // 2
CTX_BLOCKS = 4
QUARTER = 4 * P
GATE_I, GATE_F, GATE_U, GATE_O = 0, 1, 2, 3
GATE_ORDER = (GATE_F, GATE_I, GATE_U, GATE_O)
WARM_UP = 3

FLOPS = 2 * 512 * SAMPLES * (P + CTX_BLOCKS * P + P)


def tile_test_target_kernel(tc, table, w_p, ctx, w_ctx, h0, u, c0, b, offs, out):
    nc = tc.nc
    with (
        tc.tile_pool(name="held", bufs=1) as held,
        tc.psum_pool(name="gates", bufs=1) as gates,
        tc.psum_pool(name="turns", bufs=4) as turns,
    ):
        zeros = held.tile([P, SAMPLES], BF16, name="zeros")
        nc.gpsimd.memset(zeros[:], 0.0)
        unread = gates.tile([P, SAMPLES], F32, name="unread")
        for i in range(WARM_UP):
            nc.tensor.matmul(unread[:], zeros[:, 0:P], zeros[:], start=True, stop=True)

        identity = held.tile([P, P], BF16, name="identity")
        make_identity(nc, identity[:])

        ctx_sb, w_ctx_sb = [], []
        for k in range(CTX_BLOCKS):
            ctx_k = held.tile([P, SAMPLES], BF16, name=f"ctx{k}")
            nc.sync.dma_start(ctx_k[:], ctx[k * P : (k + 1) * P, :])
            ctx_sb.append(ctx_k)
            w_ctx_k = held.tile([P, 4 * P], BF16, name=f"w_ctx{k}")
            nc.scalar.dma_start(w_ctx_k[:], w_ctx[k * P : (k + 1) * P, :])
            w_ctx_sb.append(w_ctx_k)
        h0_sb = held.tile([P, SAMPLES], BF16, name="h0_sb")
        nc.sync.dma_start(h0_sb[:], h0)
        u_sb = held.tile([P, 4 * P], BF16, name="u_sb")
        nc.scalar.dma_start(u_sb[:], u)

        table_blocks = table.rearrange("(t p) d -> p t d", p=P)
        rows = []
        for q in range(4):
            rows_q = held.tile([P, 4, P], BF16, name=f"rows{q}")
            queue = nc.sync if q % 2 == 0 else nc.scalar
            queue.dma_start(rows_q[:], table_blocks[:, 4 * q : 4 * (q + 1), :])
            rows.append(rows_q)

        offsets = held.tile([P, SAMPLES // 16], U16, name="offsets")
        nc.sync.dma_start(offsets[:], offs)
        w_p_sb = held.tile([P, 4 * P], BF16, name="w_p_sb")
        nc.scalar.dma_start(w_p_sb[:], w_p)
        c0_sb = held.tile([P, SAMPLES], F32, name="c0_sb")
        nc.sync.dma_start(c0_sb[:], c0)
        b_sb = held.tile([P, 4], F32, name="b_sb")
        with nc.allow_non_contiguous_dma(reason="512 floats, one to a partition and gate"):
            nc.gpsimd.dma_start(b_sb[:], b.rearrange("(g p) o -> p (g o)", p=P))

        def gate_columns(g):
            return slice(g * P, (g + 1) * P)

        z = {}

        def context(g, blocks):
            for k in blocks:
                nc.tensor.matmul(
                    z[g][:], w_ctx_sb[k][:, gate_columns(g)], ctx_sb[k][:], start=(k == 0), stop=False
                )

        def hidden(g, last):
            nc.tensor.matmul(z[g][:], u_sb[:, gate_columns(g)], h0_sb[:], start=False, stop=last)

        def looked_up(g, last):
            for half in range(2):
                nc.tensor.matmul(
                    z[g][:, half * HALF : (half + 1) * HALF],
                    w_p_sb[:, gate_columns(g)],
                    speakers[:].indirect(offsets[:, half * (HALF // 16) : (half + 1) * (HALF // 16)]),
                    start=False,
                    stop=(last and half == 1),
                )

        for g in (GATE_F, GATE_I, GATE_U):
            z[g] = gates.tile([P, SAMPLES], F32, name=f"z{g}")
            context(g, range(CTX_BLOCKS))
            hidden(g, last=False)

        speakers = held.tile([P, SPEAKERS], BF16, name="speakers")
        for q in range(4):
            flipped = turns.tile([P, QUARTER], BF16, name="flipped", tag="turn")
            for t in range(4):
                nc.tensor.transpose(flipped[:, t * P : (t + 1) * P], rows[q][:, t, :], identity[:])
            nc.vector.tensor_copy(speakers[:, q * QUARTER : (q + 1) * QUARTER], flipped[:])

        z[GATE_O] = turns.tile([P, SAMPLES], F32, name="z_o", tag="turn")
        context(GATE_O, range(CTX_BLOCKS - 1))
        for g in GATE_ORDER:
            looked_up(g, last=(g != GATE_O))
        context(GATE_O, [CTX_BLOCKS - 1])
        hidden(GATE_O, last=True)

        def bias(g):
            return b_sb[:, g : g + 1]

        forget = held.tile([P, SAMPLES], F32, name="forget")
        nc.scalar.activation(forget[:], z[GATE_F][:], FUNC.Sigmoid, bias=bias(GATE_F))
        kept = held.tile([P, SAMPLES], F32, name="kept")
        nc.vector.tensor_tensor(kept[:], forget[:], c0_sb[:], ALU.mult)

        admit = held.tile([P, SAMPLES], F32, name="admit")
        nc.scalar.activation(admit[:], z[GATE_I][:], FUNC.Sigmoid, bias=bias(GATE_I))
        fresh = held.tile([P, SAMPLES], F32, name="fresh")
        nc.vector.scalar_tensor_tensor(fresh[:], z[GATE_U][:], bias(GATE_U), admit[:], ALU.add, ALU.mult)
        c1 = held.tile([P, SAMPLES], F32, name="c1")
        nc.vector.scalar_tensor_tensor(c1[:], fresh[:], 0.0, kept[:], ALU.max, ALU.add)
        nc.sync.dma_start(out[P : 2 * P, :], c1[:])

        expose = held.tile([P, SAMPLES], F32, name="expose")
        h1 = held.tile([P, SAMPLES], F32, name="h1")
        for half in range(2):
            cols = slice(half * HALF, (half + 1) * HALF)
            nc.scalar.activation(expose[:, cols], z[GATE_O][:, cols], FUNC.Sigmoid, bias=bias(GATE_O))
            nc.vector.scalar_tensor_tensor(h1[:, cols], c1[:, cols], 0.0, expose[:, cols], ALU.max, ALU.mult)
            queue = nc.scalar if half == 0 else nc.sync
            queue.dma_start(out[0:P, cols], h1[:, cols])
